import numpy as np
import ml_dtypes


def mxq(x, axis, fmt="e4m3"):
    dtype, down = {"e4m3": (ml_dtypes.float8_e4m3fn, 7), "e5m2": (ml_dtypes.float8_e5m2, 14)}[fmt]
    v = np.moveaxis(np.asarray(x, np.float32).astype(ml_dtypes.bfloat16).astype(np.float64), axis, -1)
    blocks = v.reshape(v.shape[:-1] + (-1, 32))
    amax = np.abs(blocks).max(-1, keepdims=True)
    byte = np.maximum(np.where(amax > 0, np.frexp(amax)[1] - 1 + 127, 0) - down, 1)
    scale = np.exp2(byte - 127.0)
    codes = (blocks / scale).astype(np.float32).astype(dtype).astype(np.float64)
    return np.moveaxis((codes * scale).reshape(v.shape), -1, axis)


WIDE = False


def mx_kscale(k):
    if not WIDE:
        return np.ones(k)
    levels = np.array([10, -10, 5, -5, 0])
    a = np.random.permutation(np.resize(levels, k // 512 * 4)).reshape(k // 512, 4)
    idx = np.arange(k)
    return np.exp2(a[idx // 512, idx % 128 // 32])


BF16 = ml_dtypes.bfloat16


def bf(x):
    return np.asarray(x, np.float32).astype(BF16)


def f64(x):
    return np.asarray(x).astype(np.float64)


B, T, D, NH, N_MLP = 4, 1024, 512, 16, 512
LN_EPS = 1e-6


def layer_norm(v, g, b):
    mu = v.mean(-1, keepdims=True)
    var = np.square(v - mu).mean(-1, keepdims=True)
    return (v - mu) / np.sqrt(var + LN_EPS) * g + b


def erf(v):
    z = np.clip(v, -6.0, 6.0)
    r = 2.0 * z * z
    term = z.copy()
    total = z.copy()
    for n in range(1, 120):
        term = term * r / (2.0 * n + 1.0)
        total = total + term
    return 2.0 / np.sqrt(np.pi) * np.exp(-z * z) * total


def gelu_erf(v):
    return 0.5 * v * (1.0 + erf(v / np.sqrt(2.0)))


def setup_inputs():
    s, t = mx_kscale(D), mx_kscale(D)
    return {"attn_out": bf(np.random.standard_normal((B, T, D)) * 0.25 * s),
            "x": bf(np.random.standard_normal((B, T, D)) * 1.5 + np.random.standard_normal((B, T, 1)) * 0.5),
            "W_proj": bf(np.random.standard_normal((D, D)) * 3.0 / np.sqrt(D) / s),
            "b_proj": bf(np.random.standard_normal(D) * 0.2),
            "g2": bf((1.0 + 0.1 * np.random.standard_normal(D)) * t),
            "beta2": bf(0.1 * np.random.standard_normal(D) * t),
            "W1": bf(np.random.standard_normal((N_MLP, D)) / np.sqrt(D) / t),
            "b1": bf(np.random.standard_normal(N_MLP) * 0.2)}


def reference(attn_out, x, W_proj, b_proj, g2, beta2, W1, b1):
    o = (mxq(f64(attn_out), 2, "e4m3") @ mxq(f64(W_proj), 1, "e4m3").T) + f64(b_proj)
    x_mid = f64(x) + o
    h = layer_norm(x_mid, f64(g2), f64(beta2))
    u = gelu_erf((mxq(h, 2, "e4m3") @ mxq(f64(W1), 1, "e4m3").T) + f64(b1))
    return x_mid, u

@@ -1,0 +1,347 @@
+from contextlib import ExitStack
+
+import concourse.mybir as mybir
+from concourse.masks import make_identity
+
+F32 = mybir.dt.float32
+BF16 = mybir.dt.bfloat16
+U32 = mybir.dt.uint32
+U8 = mybir.dt.uint8
+FP8X4 = mybir.dt.float8_e4m3fn_x4
+ALU = mybir.AluOpType
+ACT = mybir.ActivationFunctionType
+
+P = 128
+PACK = 4
+D = P * PACK
+TOKENS = 4 * 1024
+GROUP_TILES = 4
+GROUP_TOKENS = GROUP_TILES * P
+HALF = GROUP_TOKENS // 2
+GROUPS = TOKENS // GROUP_TOKENS
+LN_EPS = 1e-6
+
+BIAS_TILES_ON_GPSIMD = 3
+
+LOAD_AHEAD = 4
+LAG = GROUPS - 2 + 3
+
+FLOPS = 2 * 2 * TOKENS * D * D
+
+
+def tile_block_pb_t_kernel(tc, attn_out, x, W_proj, b_proj, g2, beta2, W1, b1, out_0, out_1):
+    nc = tc.nc
+
+    def by_group(rows):
+        return rows.flatten_outer_dims().rearrange("(g p j) d -> g p j d", p=P, j=GROUP_TILES)
+
+    attn_groups, x_groups = by_group(attn_out), by_group(x)
+    x_mid_groups, u_groups = by_group(out_0), by_group(out_1)
+
+    with ExitStack() as ctx:
+        const = ctx.enter_context(tc.tile_pool(name="const", bufs=1))
+        resident = ctx.enter_context(tc.tile_pool(name="resident", bufs=1))
+        inputs = ctx.enter_context(tc.tile_pool(name="inputs", bufs=LOAD_AHEAD))
+        pairs = ctx.enter_context(tc.tile_pool(name="pairs", bufs=2))
+        triples = ctx.enter_context(tc.tile_pool(name="triples", bufs=3))
+        flipped = ctx.enter_context(tc.psum_pool(name="flipped", bufs=4))
+        sums = ctx.enter_context(tc.psum_pool(name="sums", bufs=4))
+
+        warm = const.tile([P, 1], F32)
+        nc.vector.memset(warm[:], 0.0)
+        nc.scalar.activation(out=warm[:], in_=warm[:], func=ACT.Gelu)
+
+        ident_f32 = const.tile([P, P], F32)
+        make_identity(nc, ident_f32[:])
+        ident_bf16 = const.tile([P, P], BF16)
+        make_identity(nc, ident_bf16[:])
+        ones = const.tile([P, P], BF16)
+        nc.vector.memset(ones[:], 1.0)
+        neg_half = const.tile([P, GROUP_TILES], F32)
+        nc.vector.memset(neg_half[:], -0.5)
+
+        row_sum = const.tile([P, GROUPS * GROUP_TILES], F32)
+        neg_mean = const.tile([P, GROUPS * GROUP_TILES], F32)
+        sq_sum = const.tile([P, GROUPS * GROUP_TILES], F32)
+        var_eps = const.tile([P, GROUPS * GROUP_TILES], F32)
+        rstd = const.tile([P, GROUPS * GROUP_TILES], F32)
+
+        attn_rows, x_rows = {}, {}
+
+        def load(g):
+            if not 0 <= g < GROUPS:
+                return
+            attn_rows[g] = inputs.tile([P, GROUP_TILES, D], BF16, name="attn_rows")
+            nc.sync.dma_start(out=attn_rows[g][:], in_=attn_groups[g])
+            x_rows[g] = inputs.tile([P, GROUP_TILES, D], BF16, name="x_rows")
+            nc.sync.dma_start(out=x_rows[g][:], in_=x_groups[g])
+
+        wp_rows = const.tile([P, PACK, D], BF16)
+        nc.sync.dma_start(out=wp_rows[:], in_=W_proj.rearrange("(c p) k -> p c k", p=P))
+        load(0)
+        load(1)
+        w1_rows = const.tile([P, PACK, D], BF16)
+        nc.sync.dma_start(out=w1_rows[:], in_=W1.rearrange("(c p) k -> p c k", p=P))
+
+        bias_rows = const.tile([P, 2, D], BF16)
+        nc.vector.memset(bias_rows[:], 0.0)
+        nc.scalar.dma_start(out=bias_rows[0:1, 0, :], in_=b_proj.rearrange("(o d) -> o d", o=1))
+        nc.scalar.dma_start(out=bias_rows[0:1, 1, :], in_=b1.rearrange("(o d) -> o d", o=1))
+        ln_rows = const.tile([P, P], BF16)
+        nc.vector.memset(ln_rows[:], 0.0)
+        nc.scalar.dma_start(out=ln_rows[0:PACK, :], in_=g2.rearrange("(t p) -> t p", p=P))
+        nc.scalar.dma_start(out=ln_rows[PACK : 2 * PACK, :], in_=beta2.rearrange("(t p) -> t p", p=P))
+
+        bias_bcast = const.tile([P, 2, D], F32)
+        for i in range(2):
+            spread = sums.tile([P, D], F32, name="acc")
+            nc.tensor.matmul(out=spread[:], lhsT=ones[:], rhs=bias_rows[:, i, :], start=True, stop=True)
+            nc.vector.tensor_copy(out=bias_bcast[:, i, :], in_=spread[:])
+
+        ln_flipped = flipped.tile([P, P], BF16, name="bank")
+        nc.tensor.transpose(ln_flipped[:], ln_rows[:], ident_bf16[:])
+        ln_cols = const.tile([P, 2 * PACK], F32)
+        nc.vector.tensor_copy(out=ln_cols[:], in_=ln_flipped[:, 0 : 2 * PACK])
+
+        def flip_words(rows, grouped):
+            row_words = rows.bitcast(F32)
+            grouped_words = grouped.bitcast(F32)
+            for half in range(2):
+                bank = flipped.tile([P, 2, HALF], F32, name="bank")
+                for jj in range(2):
+                    for u in range(2):
+                        nc.tensor.transpose(
+                            bank[:, u, jj * P : (jj + 1) * P],
+                            row_words[:, 2 * half + jj, u * P : (u + 1) * P],
+                            ident_f32[:],
+                        )
+                nc.scalar.copy(
+                    out=grouped_words[:, half * HALF : (half + 1) * HALF, :],
+                    in_=bank[:].rearrange("p u w -> p w u"),
+                )
+
+        def quantise(grouped, codes, scales):
+            nc.vector.quantize_mx(
+                out=codes.bitcast(FP8X4), scales=scales, in_=grouped.rearrange("p w t -> p (w t)")
+            )
+
+        def mx_operand(pool, name):
+            codes = pool.tile([P, GROUP_TOKENS], U32, name=name + "_codes", align_bytes=64)
+            scales = pool.tile([P, GROUP_TOKENS], U8, name=name + "_scales", align_bytes=64)
+            return codes, scales
+
+        wp_grouped = pairs.tile([P, D, PACK], BF16, name="a_grouped", align_bytes=64)
+        flip_words(wp_rows[:], wp_grouped[:])
+        wp_codes, wp_scales = mx_operand(const, "wp")
+        quantise(wp_grouped[:], wp_codes[:], wp_scales[:])
+
+        w1_codes, w1_scales = mx_operand(const, "w1")
+
+        def prepare_w1():
+            w1_grouped = pairs.tile([P, D, PACK], BF16, name="h_grouped", align_bytes=64)
+            for half in range(2):
+                bank = flipped.tile([P, PACK, HALF], BF16, name="bank")
+                for cc in range(2):
+                    for t in range(PACK):
+                        nc.tensor.transpose(
+                            bank[:, t, cc * P : (cc + 1) * P],
+                            w1_rows[:, 2 * half + cc, t * P : (t + 1) * P],
+                            ident_bf16[:],
+                        )
+                nc.vector.tensor_copy(
+                    out=w1_grouped[:, half * HALF : (half + 1) * HALF, :],
+                    in_=bank[:].rearrange("p t n -> p n t"),
+                )
+            quantise(w1_grouped[:], w1_codes[:], w1_scales[:])
+
+        a_grouped, a_operand, x_mid = {}, {}, {}
+
+        def stat_cols(g):
+            return slice(g * GROUP_TILES, (g + 1) * GROUP_TILES)
+
+        def stat_col(g, j):
+            return slice(g * GROUP_TILES + j, g * GROUP_TILES + j + 1)
+
+        def add_bias(g):
+            if not 0 <= g < GROUPS:
+                return
+            x_mid[g] = resident.tile([P, GROUP_TILES, D], F32, name="x_mid_%d" % g)
+            split = BIAS_TILES_ON_GPSIMD
+            nc.gpsimd.tensor_tensor(
+                out=x_mid[g][:, 0:split, :],
+                in0=x_rows[g][:, 0:split, :],
+                in1=bias_bcast[:, 0:1, :].to_broadcast([P, split, D]),
+                op=ALU.add,
+            )
+            nc.vector.tensor_tensor(
+                out=x_mid[g][:, split:GROUP_TILES, :],
+                in0=x_rows[g][:, split:GROUP_TILES, :],
+                in1=bias_bcast[:, 0:1, :].to_broadcast([P, GROUP_TILES - split, D]),
+                op=ALU.add,
+            )
+
+        def flip_attention(g):
+            if not 0 <= g < GROUPS:
+                return
+            a_grouped[g] = pairs.tile([P, GROUP_TOKENS, PACK], BF16, name="a_grouped", align_bytes=64)
+            flip_words(attn_rows[g][:], a_grouped[g][:])
+
+        def quantise_attention(g):
+            if not 0 <= g < GROUPS:
+                return
+            a_operand[g] = mx_operand(pairs, "a")
+            quantise(a_grouped[g][:], a_operand[g][0][:], a_operand[g][1][:])
+
+        def project_attention(g):
+            if not 0 <= g < GROUPS:
+                return
+            codes, scales = a_operand[g]
+            for j in range(GROUP_TILES):
+                tokens = slice(j * P, (j + 1) * P)
+                acc = sums.tile([P, D], F32, name="acc")
+                nc.tensor.matmul_mx(
+                    out=acc[:],
+                    lhsT=codes[:, tokens].bitcast(FP8X4),
+                    lhsT_scale=scales[:, tokens],
+                    rhs=wp_codes[:].bitcast(FP8X4),
+                    rhs_scale=wp_scales[:],
+                    start=True,
+                    stop=True,
+                )
+                nc.vector.scalar_tensor_tensor(
+                    out=x_mid[g][:, j, :],
+                    in0=acc[:],
+                    scalar=1.0,
+                    in1=x_mid[g][:, j, :],
+                    op0=ALU.mult,
+                    op1=ALU.add,
+                    accum_out=row_sum[:, stat_col(g, j)],
+                )
+            nc.vector.tensor_scalar(
+                out=neg_mean[:, stat_cols(g)],
+                in0=row_sum[:, stat_cols(g)],
+                scalar1=-1.0 / D,
+                scalar2=None,
+                op0=ALU.mult,
+            )
+
+        def variance(g):
+            if not 0 <= g < GROUPS:
+                return
+            squares = pairs.tile([P, GROUP_TILES, D], BF16, name="squares")
+            for j in range(GROUP_TILES):
+                nc.scalar.activation(
+                    out=squares[:, j, :],
+                    in_=x_mid[g][:, j, :],
+                    func=ACT.Square,
+                    bias=neg_mean[:, stat_col(g, j)],
+                    scale=1.0,
+                    accum_out=sq_sum[:, stat_col(g, j)],
+                )
+            nc.scalar.dma_start(out=x_mid_groups[g], in_=x_mid[g][:])
+
+        def reciprocal_std(g):
+            if not 0 <= g < GROUPS:
+                return
+            nc.gpsimd.tensor_scalar(
+                out=var_eps[:, stat_cols(g)],
+                in0=sq_sum[:, stat_cols(g)],
+                scalar1=1.0 / D,
+                scalar2=LN_EPS,
+                op0=ALU.mult,
+                op1=ALU.add,
+            )
+            nc.gpsimd.tensor_tensor(
+                out=rstd[:, stat_cols(g)], in0=var_eps[:, stat_cols(g)], in1=neg_half[:], op=ALU.pow
+            )
+
+        normed, h_planes, h_grouped, h_operand, hidden = {}, {}, {}, {}, {}
+
+        def normalise(g):
+            if not 0 <= g < GROUPS:
+                return
+            normed[g] = triples.tile([P, GROUP_TILES, D], F32, name="normed")
+            for j in range(GROUP_TILES):
+                nc.gpsimd.tensor_scalar(
+                    out=normed[g][:, j, :],
+                    in0=x_mid[g][:, j, :],
+                    scalar1=neg_mean[:, stat_col(g, j)],
+                    scalar2=rstd[:, stat_col(g, j)],
+                    op0=ALU.add,
+                    op1=ALU.mult,
+                )
+
+        def flip_normed(g):
+            if not 0 <= g < GROUPS:
+                return
+            h_planes[g] = pairs.tile([P, PACK, GROUP_TOKENS], BF16, name="h_planes")
+            for t in range(PACK):
+                bank = flipped.tile([P, GROUP_TOKENS], F32, name="bank")
+                for j in range(GROUP_TILES):
+                    nc.tensor.transpose(
+                        bank[:, j * P : (j + 1) * P], normed[g][:, j, t * P : (t + 1) * P], ident_f32[:]
+                    )
+                nc.scalar.activation(
+                    out=h_planes[g][:, t, :],
+                    in_=bank[:],
+                    func=ACT.Identity,
+                    scale=ln_cols[:, t : t + 1],
+                    bias=ln_cols[:, PACK + t : PACK + t + 1],
+                )
+
+        def regroup_h(g):
+            if not 0 <= g < GROUPS:
+                return
+            h_grouped[g] = pairs.tile([P, GROUP_TOKENS, PACK], BF16, name="h_grouped", align_bytes=64)
+            nc.vector.tensor_copy(out=h_grouped[g][:], in_=h_planes[g][:].rearrange("p t w -> p w t"))
+
+        def quantise_h(g):
+            if not 0 <= g < GROUPS:
+                return
+            h_operand[g] = mx_operand(pairs, "h")
+            quantise(h_grouped[g][:], h_operand[g][0][:], h_operand[g][1][:])
+
+        def project_h(g):
+            if not 0 <= g < GROUPS:
+                return
+            codes, scales = h_operand[g]
+            hidden[g] = triples.tile([P, GROUP_TILES, D], F32, name="hidden")
+            for j in range(GROUP_TILES):
+                tokens = slice(j * P, (j + 1) * P)
+                acc = sums.tile([P, D], F32, name="acc")
+                nc.tensor.matmul_mx(
+                    out=acc[:],
+                    lhsT=codes[:, tokens].bitcast(FP8X4),
+                    lhsT_scale=scales[:, tokens],
+                    rhs=w1_codes[:].bitcast(FP8X4),
+                    rhs_scale=w1_scales[:],
+                    start=True,
+                    stop=True,
+                )
+                nc.vector.tensor_tensor(
+                    out=hidden[g][:, j, :], in0=acc[:], in1=bias_bcast[:, 1, :], op=ALU.add
+                )
+
+        def gelu(g):
+            if not 0 <= g < GROUPS:
+                return
+            nc.scalar.activation(out=hidden[g][:], in_=hidden[g][:], func=ACT.Gelu)
+            nc.scalar.dma_start(out=u_groups[g], in_=hidden[g][:])
+
+        for step in range(-2, LAG + GROUPS + 1):
+            late = step - LAG
+            load(step + LOAD_AHEAD)
+            project_attention(step)
+            variance(step - 1)
+            regroup_h(late + 1)
+            project_h(late)
+            gelu(late - 1)
+            add_bias(step + 2)
+            normalise(late + 3)
+            reciprocal_std(step - 1)
+            flip_attention(step + 1)
+            if step == GROUPS - 2:
+                prepare_w1()
+            flip_normed(late + 2)
+            quantise_attention(step + 1)
+            quantise_h(late + 1)

@@ -328,20 +328,21 @@ def tile_block_pb_t_kernel(tc, attn_out, x, W_proj, b_proj, g2, beta2, W1, b1, o
             nc.scalar.activation(out=hidden[g][:], in_=hidden[g][:], func=ACT.Gelu)
             nc.scalar.dma_start(out=u_groups[g], in_=hidden[g][:])
 
-        for step in range(-2, LAG + GROUPS + 1):
-            late = step - LAG
-            load(step + LOAD_AHEAD)
-            project_attention(step)
-            variance(step - 1)
-            regroup_h(late + 1)
-            project_h(late)
-            gelu(late - 1)
-            add_bias(step + 2)
-            normalise(late + 3)
-            reciprocal_std(step - 1)
-            flip_attention(step + 1)
-            if step == GROUPS - 2:
-                prepare_w1()
-            flip_normed(late + 2)
-            quantise_attention(step + 1)
-            quantise_h(late + 1)
+        with tc.manual_schedule():
+            for step in range(-2, LAG + GROUPS + 1):
+                late = step - LAG
+                load(step + LOAD_AHEAD)
+                project_attention(step)
+                variance(step - 1)
+                regroup_h(late + 1)
+                project_h(late)
+                gelu(late - 1)
+                add_bias(step + 2)
+                normalise(late + 3)
+                reciprocal_std(step - 1)
+                flip_attention(step + 1)
+                if step == GROUPS - 2:
+                    prepare_w1()
+                flip_normed(late + 2)
+                quantise_attention(step + 1)
+                quantise_h(late + 1)

@@ -21,8 +21,6 @@ HALF = GROUP_TOKENS // 2
 GROUPS = TOKENS // GROUP_TOKENS
 LN_EPS = 1e-6
 
-BIAS_TILES_ON_GPSIMD = 3
-
 LOAD_AHEAD = 4
 LAG = GROUPS - 2 + 3
 
@@ -166,17 +164,10 @@ def tile_block_pb_t_kernel(tc, attn_out, x, W_proj, b_proj, g2, beta2, W1, b1, o
             if not 0 <= g < GROUPS:
                 return
             x_mid[g] = resident.tile([P, GROUP_TILES, D], F32, name="x_mid_%d" % g)
-            split = BIAS_TILES_ON_GPSIMD
-            nc.gpsimd.tensor_tensor(
-                out=x_mid[g][:, 0:split, :],
-                in0=x_rows[g][:, 0:split, :],
-                in1=bias_bcast[:, 0:1, :].to_broadcast([P, split, D]),
-                op=ALU.add,
-            )
             nc.vector.tensor_tensor(
-                out=x_mid[g][:, split:GROUP_TILES, :],
-                in0=x_rows[g][:, split:GROUP_TILES, :],
-                in1=bias_bcast[:, 0:1, :].to_broadcast([P, GROUP_TILES - split, D]),
+                out=x_mid[g][:],
+                in0=x_rows[g][:],
+                in1=bias_bcast[:, 0:1, :].to_broadcast([P, GROUP_TILES, D]),
                 op=ALU.add,
             )
 
@@ -262,7 +253,7 @@ def tile_block_pb_t_kernel(tc, attn_out, x, W_proj, b_proj, g2, beta2, W1, b1, o
                 return
             normed[g] = triples.tile([P, GROUP_TILES, D], F32, name="normed")
             for j in range(GROUP_TILES):
-                nc.gpsimd.tensor_scalar(
+                nc.vector.tensor_scalar(
                     out=normed[g][:, j, :],
                     in0=x_mid[g][:, j, :],
                     scalar1=neg_mean[:, stat_col(g, j)],

@@ -19,10 +19,8 @@ GROUP_TILES = 4
 GROUP_TOKENS = GROUP_TILES * P
 HALF = GROUP_TOKENS // 2
 GROUPS = TOKENS // GROUP_TOKENS
+STAT_COLS = GROUPS * GROUP_TILES
 LN_EPS = 1e-6
-
-LOAD_AHEAD = 4
-LAG = GROUPS - 2 + 3
 
 FLOPS = 2 * 2 * TOKENS * D * D
 
@@ -37,13 +35,41 @@ def tile_block_pb_t_kernel(tc, attn_out, x, W_proj, b_proj, g2, beta2, W1, b1, o
     x_mid_groups, u_groups = by_group(out_0), by_group(out_1)
 
     with ExitStack() as ctx:
+        ctx.enter_context(tc.manual_schedule())
         const = ctx.enter_context(tc.tile_pool(name="const", bufs=1))
         resident = ctx.enter_context(tc.tile_pool(name="resident", bufs=1))
-        inputs = ctx.enter_context(tc.tile_pool(name="inputs", bufs=LOAD_AHEAD))
+        inputs = ctx.enter_context(tc.tile_pool(name="inputs", bufs=4))
         pairs = ctx.enter_context(tc.tile_pool(name="pairs", bufs=2))
         triples = ctx.enter_context(tc.tile_pool(name="triples", bufs=3))
         flipped = ctx.enter_context(tc.psum_pool(name="flipped", bufs=4))
         sums = ctx.enter_context(tc.psum_pool(name="sums", bufs=4))
+
+        attn_rows, x_rows = {}, {}
+
+        def load(g):
+            if not 0 <= g < GROUPS:
+                return
+            attn_rows[g] = inputs.tile([P, GROUP_TILES, D], BF16, name="attn_rows")
+            nc.sync.dma_start(out=attn_rows[g][:], in_=attn_groups[g])
+            x_rows[g] = inputs.tile([P, GROUP_TILES, D], BF16, name="x_rows")
+            nc.sync.dma_start(out=x_rows[g][:], in_=x_groups[g])
+
+        bias_rows = const.tile([P, 2, D], BF16)
+        nc.vector.memset(bias_rows[:], 0.0)
+        ln_rows = const.tile([P, P], BF16)
+        nc.vector.memset(ln_rows[:], 0.0)
+        nc.scalar.dma_start(out=bias_rows[0:1, 0, :], in_=b_proj.rearrange("(o d) -> o d", o=1))
+        nc.scalar.dma_start(out=bias_rows[0:1, 1, :], in_=b1.rearrange("(o d) -> o d", o=1))
+        nc.scalar.dma_start(out=ln_rows[0:PACK, :], in_=g2.rearrange("(t p) -> t p", p=P))
+        nc.scalar.dma_start(out=ln_rows[PACK : 2 * PACK, :], in_=beta2.rearrange("(t p) -> t p", p=P))
+
+        wp_rows = const.tile([P, PACK, D], BF16)
+        nc.sync.dma_start(out=wp_rows[:], in_=W_proj.rearrange("(c p) k -> p c k", p=P))
+        load(0)
+        load(1)
+        load(2)
+        w1_rows = const.tile([P, PACK, D], BF16)
+        nc.sync.dma_start(out=w1_rows[:], in_=W1.rearrange("(c p) k -> p c k", p=P))
 
         warm = const.tile([P, 1], F32)
         nc.vector.memset(warm[:], 0.0)
@@ -58,52 +84,32 @@ def tile_block_pb_t_kernel(tc, attn_out, x, W_proj, b_proj, g2, beta2, W1, b1, o
         neg_half = const.tile([P, GROUP_TILES], F32)
         nc.vector.memset(neg_half[:], -0.5)
 
-        row_sum = const.tile([P, GROUPS * GROUP_TILES], F32)
-        neg_mean = const.tile([P, GROUPS * GROUP_TILES], F32)
-        sq_sum = const.tile([P, GROUPS * GROUP_TILES], F32)
-        var_eps = const.tile([P, GROUPS * GROUP_TILES], F32)
-        rstd = const.tile([P, GROUPS * GROUP_TILES], F32)
+        row_sum = const.tile([P, STAT_COLS], F32)
+        neg_mean = const.tile([P, STAT_COLS], F32)
+        sq_sum = const.tile([P, STAT_COLS], F32)
+        var_eps = const.tile([P, STAT_COLS], F32)
+        rstd = const.tile([P, STAT_COLS], F32)
 
-        attn_rows, x_rows = {}, {}
+        def stat_cols(g):
+            return slice(g * GROUP_TILES, (g + 1) * GROUP_TILES)
 
-        def load(g):
-            if not 0 <= g < GROUPS:
-                return
-            attn_rows[g] = inputs.tile([P, GROUP_TILES, D], BF16, name="attn_rows")
-            nc.sync.dma_start(out=attn_rows[g][:], in_=attn_groups[g])
-            x_rows[g] = inputs.tile([P, GROUP_TILES, D], BF16, name="x_rows")
-            nc.sync.dma_start(out=x_rows[g][:], in_=x_groups[g])
-
-        wp_rows = const.tile([P, PACK, D], BF16)
-        nc.sync.dma_start(out=wp_rows[:], in_=W_proj.rearrange("(c p) k -> p c k", p=P))
-        load(0)
-        load(1)
-        w1_rows = const.tile([P, PACK, D], BF16)
-        nc.sync.dma_start(out=w1_rows[:], in_=W1.rearrange("(c p) k -> p c k", p=P))
-
-        bias_rows = const.tile([P, 2, D], BF16)
-        nc.vector.memset(bias_rows[:], 0.0)
-        nc.scalar.dma_start(out=bias_rows[0:1, 0, :], in_=b_proj.rearrange("(o d) -> o d", o=1))
-        nc.scalar.dma_start(out=bias_rows[0:1, 1, :], in_=b1.rearrange("(o d) -> o d", o=1))
-        ln_rows = const.tile([P, P], BF16)
-        nc.vector.memset(ln_rows[:], 0.0)
-        nc.scalar.dma_start(out=ln_rows[0:PACK, :], in_=g2.rearrange("(t p) -> t p", p=P))
-        nc.scalar.dma_start(out=ln_rows[PACK : 2 * PACK, :], in_=beta2.rearrange("(t p) -> t p", p=P))
+        def stat_col(g, j):
+            return slice(g * GROUP_TILES + j, g * GROUP_TILES + j + 1)
 
         bias_bcast = const.tile([P, 2, D], F32)
         for i in range(2):
             spread = sums.tile([P, D], F32, name="acc")
             nc.tensor.matmul(out=spread[:], lhsT=ones[:], rhs=bias_rows[:, i, :], start=True, stop=True)
-            nc.vector.tensor_copy(out=bias_bcast[:, i, :], in_=spread[:])
+            nc.scalar.copy(out=bias_bcast[:, i, :], in_=spread[:])
 
         ln_flipped = flipped.tile([P, P], BF16, name="bank")
         nc.tensor.transpose(ln_flipped[:], ln_rows[:], ident_bf16[:])
         ln_cols = const.tile([P, 2 * PACK], F32)
-        nc.vector.tensor_copy(out=ln_cols[:], in_=ln_flipped[:, 0 : 2 * PACK])
+        nc.scalar.copy(out=ln_cols[:], in_=ln_flipped[:, 0 : 2 * PACK])
 
-        def flip_words(rows, grouped):
+        def flip_words(rows):
             row_words = rows.bitcast(F32)
-            grouped_words = grouped.bitcast(F32)
+            banks = []
             for half in range(2):
                 bank = flipped.tile([P, 2, HALF], F32, name="bank")
                 for jj in range(2):
@@ -113,14 +119,21 @@ def tile_block_pb_t_kernel(tc, attn_out, x, W_proj, b_proj, g2, beta2, W1, b1, o
                             row_words[:, 2 * half + jj, u * P : (u + 1) * P],
                             ident_f32[:],
                         )
+                banks.append(bank)
+            return banks
+
+        def copy_words(banks, grouped):
+            grouped_words = grouped.bitcast(F32)
+            for half in range(2):
                 nc.scalar.copy(
                     out=grouped_words[:, half * HALF : (half + 1) * HALF, :],
-                    in_=bank[:].rearrange("p u w -> p w u"),
+                    in_=banks[half][:].rearrange("p u w -> p w u"),
                 )
 
-        def quantise(grouped, codes, scales):
+        def quantise(grouped, operand):
+            codes, scales = operand
             nc.vector.quantize_mx(
-                out=codes.bitcast(FP8X4), scales=scales, in_=grouped.rearrange("p w t -> p (w t)")
+                out=codes[:].bitcast(FP8X4), scales=scales[:], in_=grouped.rearrange("p w t -> p (w t)")
             )
 
         def mx_operand(pool, name):
@@ -128,15 +141,27 @@ def tile_block_pb_t_kernel(tc, attn_out, x, W_proj, b_proj, g2, beta2, W1, b1, o
             scales = pool.tile([P, GROUP_TOKENS], U8, name=name + "_scales", align_bytes=64)
             return codes, scales
 
+        def matmul_mx_tile(acc, tokens_operand, j, weight_operand):
+            tokens = slice(j * P, (j + 1) * P)
+            nc.tensor.matmul_mx(
+                out=acc[:],
+                lhsT=tokens_operand[0][:, tokens].bitcast(FP8X4),
+                lhsT_scale=tokens_operand[1][:, tokens],
+                rhs=weight_operand[0][:].bitcast(FP8X4),
+                rhs_scale=weight_operand[1][:],
+                start=True,
+                stop=True,
+            )
+
         wp_grouped = pairs.tile([P, D, PACK], BF16, name="a_grouped", align_bytes=64)
-        flip_words(wp_rows[:], wp_grouped[:])
-        wp_codes, wp_scales = mx_operand(const, "wp")
-        quantise(wp_grouped[:], wp_codes[:], wp_scales[:])
+        copy_words(flip_words(wp_rows[:]), wp_grouped[:])
+        wp_operand = mx_operand(const, "wp")
+        quantise(wp_grouped[:], wp_operand)
 
-        w1_codes, w1_scales = mx_operand(const, "w1")
+        w1_operand = mx_operand(const, "w1")
+        w1_grouped = const.tile([P, D, PACK], BF16, align_bytes=64)
 
-        def prepare_w1():
-            w1_grouped = pairs.tile([P, D, PACK], BF16, name="h_grouped", align_bytes=64)
+        def flip_w1():
             for half in range(2):
                 bank = flipped.tile([P, PACK, HALF], BF16, name="bank")
                 for cc in range(2):
@@ -146,19 +171,13 @@ def tile_block_pb_t_kernel(tc, attn_out, x, W_proj, b_proj, g2, beta2, W1, b1, o
                             w1_rows[:, 2 * half + cc, t * P : (t + 1) * P],
                             ident_bf16[:],
                         )
-                nc.vector.tensor_copy(
+                nc.scalar.copy(
                     out=w1_grouped[:, half * HALF : (half + 1) * HALF, :],
                     in_=bank[:].rearrange("p t n -> p n t"),
                 )
-            quantise(w1_grouped[:], w1_codes[:], w1_scales[:])
 
-        a_grouped, a_operand, x_mid = {}, {}, {}
-
-        def stat_cols(g):
-            return slice(g * GROUP_TILES, (g + 1) * GROUP_TILES)
-
-        def stat_col(g, j):
-            return slice(g * GROUP_TILES + j, g * GROUP_TILES + j + 1)
+        a_banks, a_grouped, a_operand, x_mid = {}, {}, {}, {}
+        normed, h_banks, h_planes, h_grouped, h_operand, hidden = {}, {}, {}, {}, {}, {}
 
         def add_bias(g):
             if not 0 <= g < GROUPS:
@@ -174,31 +193,26 @@ def tile_block_pb_t_kernel(tc, attn_out, x, W_proj, b_proj, g2, beta2, W1, b1, o
         def flip_attention(g):
             if not 0 <= g < GROUPS:
                 return
+            a_banks[g] = flip_words(attn_rows[g][:])
+
+        def copy_attention(g):
+            if not 0 <= g < GROUPS:
+                return
             a_grouped[g] = pairs.tile([P, GROUP_TOKENS, PACK], BF16, name="a_grouped", align_bytes=64)
-            flip_words(attn_rows[g][:], a_grouped[g][:])
+            copy_words(a_banks[g], a_grouped[g][:])
 
         def quantise_attention(g):
             if not 0 <= g < GROUPS:
                 return
-            a_operand[g] = mx_operand(pairs, "a")
-            quantise(a_grouped[g][:], a_operand[g][0][:], a_operand[g][1][:])
+            a_operand[g] = mx_operand(triples, "a")
+            quantise(a_grouped[g][:], a_operand[g])
 
         def project_attention(g):
             if not 0 <= g < GROUPS:
                 return
-            codes, scales = a_operand[g]
             for j in range(GROUP_TILES):
-                tokens = slice(j * P, (j + 1) * P)
                 acc = sums.tile([P, D], F32, name="acc")
-                nc.tensor.matmul_mx(
-                    out=acc[:],
-                    lhsT=codes[:, tokens].bitcast(FP8X4),
-                    lhsT_scale=scales[:, tokens],
-                    rhs=wp_codes[:].bitcast(FP8X4),
-                    rhs_scale=wp_scales[:],
-                    start=True,
-                    stop=True,
-                )
+                matmul_mx_tile(acc, a_operand[g], j, wp_operand)
                 nc.vector.scalar_tensor_tensor(
                     out=x_mid[g][:, j, :],
                     in0=acc[:],
@@ -208,17 +222,11 @@ def tile_block_pb_t_kernel(tc, attn_out, x, W_proj, b_proj, g2, beta2, W1, b1, o
                     op1=ALU.add,
                     accum_out=row_sum[:, stat_col(g, j)],
                 )
-            nc.vector.tensor_scalar(
-                out=neg_mean[:, stat_cols(g)],
-                in0=row_sum[:, stat_cols(g)],
-                scalar1=-1.0 / D,
-                scalar2=None,
-                op0=ALU.mult,
-            )
 
         def variance(g):
             if not 0 <= g < GROUPS:
                 return
+            nc.scalar.mul(out=neg_mean[:, stat_cols(g)], in_=row_sum[:, stat_cols(g)], mul=-1.0 / D)
             squares = pairs.tile([P, GROUP_TILES, D], BF16, name="squares")
             for j in range(GROUP_TILES):
                 nc.scalar.activation(
@@ -246,12 +254,10 @@ def tile_block_pb_t_kernel(tc, attn_out, x, W_proj, b_proj, g2, beta2, W1, b1, o
                 out=rstd[:, stat_cols(g)], in0=var_eps[:, stat_cols(g)], in1=neg_half[:], op=ALU.pow
             )
 
-        normed, h_planes, h_grouped, h_operand, hidden = {}, {}, {}, {}, {}
-
         def normalise(g):
             if not 0 <= g < GROUPS:
                 return
-            normed[g] = triples.tile([P, GROUP_TILES, D], F32, name="normed")
+            normed[g] = pairs.tile([P, GROUP_TILES, D], F32, name="normed")
             for j in range(GROUP_TILES):
                 nc.vector.tensor_scalar(
                     out=normed[g][:, j, :],
@@ -265,16 +271,23 @@ def tile_block_pb_t_kernel(tc, attn_out, x, W_proj, b_proj, g2, beta2, W1, b1, o
         def flip_normed(g):
             if not 0 <= g < GROUPS:
                 return
-            h_planes[g] = pairs.tile([P, PACK, GROUP_TOKENS], BF16, name="h_planes")
+            h_banks[g] = []
             for t in range(PACK):
                 bank = flipped.tile([P, GROUP_TOKENS], F32, name="bank")
                 for j in range(GROUP_TILES):
                     nc.tensor.transpose(
                         bank[:, j * P : (j + 1) * P], normed[g][:, j, t * P : (t + 1) * P], ident_f32[:]
                     )
+                h_banks[g].append(bank)
+
+        def scale_shift(g):
+            if not 0 <= g < GROUPS:
+                return
+            h_planes[g] = pairs.tile([P, PACK, GROUP_TOKENS], BF16, name="h_planes")
+            for t in range(PACK):
                 nc.scalar.activation(
                     out=h_planes[g][:, t, :],
-                    in_=bank[:],
+                    in_=h_banks[g][t][:],
                     func=ACT.Identity,
                     scale=ln_cols[:, t : t + 1],
                     bias=ln_cols[:, PACK + t : PACK + t + 1],
@@ -284,31 +297,24 @@ def tile_block_pb_t_kernel(tc, attn_out, x, W_proj, b_proj, g2, beta2, W1, b1, o
             if not 0 <= g < GROUPS:
                 return
             h_grouped[g] = pairs.tile([P, GROUP_TOKENS, PACK], BF16, name="h_grouped", align_bytes=64)
-            nc.vector.tensor_copy(out=h_grouped[g][:], in_=h_planes[g][:].rearrange("p t w -> p w t"))
+            nc.vector.tensor_copy(
+                out=h_grouped[g][:].rearrange("p (c i) t -> p c t i", i=4),
+                in_=h_planes[g][:].rearrange("p t (c i) -> p c t i", i=4),
+            )
 
         def quantise_h(g):
             if not 0 <= g < GROUPS:
                 return
-            h_operand[g] = mx_operand(pairs, "h")
-            quantise(h_grouped[g][:], h_operand[g][0][:], h_operand[g][1][:])
+            h_operand[g] = mx_operand(triples, "h")
+            quantise(h_grouped[g][:], h_operand[g])
 
         def project_h(g):
             if not 0 <= g < GROUPS:
                 return
-            codes, scales = h_operand[g]
             hidden[g] = triples.tile([P, GROUP_TILES, D], F32, name="hidden")
             for j in range(GROUP_TILES):
-                tokens = slice(j * P, (j + 1) * P)
                 acc = sums.tile([P, D], F32, name="acc")
-                nc.tensor.matmul_mx(
-                    out=acc[:],
-                    lhsT=codes[:, tokens].bitcast(FP8X4),
-                    lhsT_scale=scales[:, tokens],
-                    rhs=w1_codes[:].bitcast(FP8X4),
-                    rhs_scale=w1_scales[:],
-                    start=True,
-                    stop=True,
-                )
+                matmul_mx_tile(acc, h_operand[g], j, w1_operand)
                 nc.vector.tensor_tensor(
                     out=hidden[g][:, j, :], in0=acc[:], in1=bias_bcast[:, 1, :], op=ALU.add
                 )
@@ -316,24 +322,29 @@ def tile_block_pb_t_kernel(tc, attn_out, x, W_proj, b_proj, g2, beta2, W1, b1, o
         def gelu(g):
             if not 0 <= g < GROUPS:
                 return
-            nc.scalar.activation(out=hidden[g][:], in_=hidden[g][:], func=ACT.Gelu)
-            nc.scalar.dma_start(out=u_groups[g], in_=hidden[g][:])
+            for half in range(2):
+                tiles = slice(2 * half, 2 * half + 2)
+                nc.scalar.activation(out=hidden[g][:, tiles, :], in_=hidden[g][:, tiles, :], func=ACT.Gelu)
+                nc.scalar.dma_start(out=u_groups[g][:, tiles, :], in_=hidden[g][:, tiles, :])
 
-        with tc.manual_schedule():
-            for step in range(-2, LAG + GROUPS + 1):
-                late = step - LAG
-                load(step + LOAD_AHEAD)
-                project_attention(step)
-                variance(step - 1)
-                regroup_h(late + 1)
-                project_h(late)
-                gelu(late - 1)
-                add_bias(step + 2)
-                normalise(late + 3)
-                reciprocal_std(step - 1)
-                flip_attention(step + 1)
-                if step == GROUPS - 2:
-                    prepare_w1()
-                flip_normed(late + 2)
-                quantise_attention(step + 1)
-                quantise_h(late + 1)
+        W1_STEP = 2
+        for step in range(-3, GROUPS + 5):
+            project_attention(step)
+            normalise(step - 1)
+            project_h(step - 5)
+            scale_shift(step - 2)
+            copy_attention(step + 2)
+            if step == W1_STEP:
+                flip_w1()
+            variance(step)
+            quantise_h(step - 3)
+            quantise_attention(step + 2)
+            if step == W1_STEP + 1:
+                quantise(w1_grouped[:], w1_operand)
+            flip_normed(step - 1)
+            gelu(step - 5)
+            add_bias(step + 3)
+            flip_attention(step + 3)
+            reciprocal_std(step)
+            regroup_h(step - 2)
+            load(step + 6)

@@ -58,10 +58,10 @@ def tile_block_pb_t_kernel(tc, attn_out, x, W_proj, b_proj, g2, beta2, W1, b1, o
         nc.vector.memset(bias_rows[:], 0.0)
         ln_rows = const.tile([P, P], BF16)
         nc.vector.memset(ln_rows[:], 0.0)
-        nc.scalar.dma_start(out=bias_rows[0:1, 0, :], in_=b_proj.rearrange("(o d) -> o d", o=1))
-        nc.scalar.dma_start(out=bias_rows[0:1, 1, :], in_=b1.rearrange("(o d) -> o d", o=1))
-        nc.scalar.dma_start(out=ln_rows[0:PACK, :], in_=g2.rearrange("(t p) -> t p", p=P))
-        nc.scalar.dma_start(out=ln_rows[PACK : 2 * PACK, :], in_=beta2.rearrange("(t p) -> t p", p=P))
+        nc.sync.dma_start(out=bias_rows[0:1, 0, :], in_=b_proj.rearrange("(o d) -> o d", o=1))
+        nc.sync.dma_start(out=bias_rows[0:1, 1, :], in_=b1.rearrange("(o d) -> o d", o=1))
+        nc.sync.dma_start(out=ln_rows[0:PACK, :], in_=g2.rearrange("(t p) -> t p", p=P))
+        nc.sync.dma_start(out=ln_rows[PACK : 2 * PACK, :], in_=beta2.rearrange("(t p) -> t p", p=P))
 
         wp_rows = const.tile([P, PACK, D], BF16)
         nc.sync.dma_start(out=wp_rows[:], in_=W_proj.rearrange("(c p) k -> p c k", p=P))
@@ -237,7 +237,7 @@ def tile_block_pb_t_kernel(tc, attn_out, x, W_proj, b_proj, g2, beta2, W1, b1, o
                     scale=1.0,
                     accum_out=sq_sum[:, stat_col(g, j)],
                 )
-            nc.scalar.dma_start(out=x_mid_groups[g], in_=x_mid[g][:])
+            nc.sync.dma_start(out=x_mid_groups[g], in_=x_mid[g][:])
 
         def reciprocal_std(g):
             if not 0 <= g < GROUPS:
@@ -322,10 +322,9 @@ def tile_block_pb_t_kernel(tc, attn_out, x, W_proj, b_proj, g2, beta2, W1, b1, o
         def gelu(g):
             if not 0 <= g < GROUPS:
                 return
-            for half in range(2):
-                tiles = slice(2 * half, 2 * half + 2)
-                nc.scalar.activation(out=hidden[g][:, tiles, :], in_=hidden[g][:, tiles, :], func=ACT.Gelu)
-                nc.scalar.dma_start(out=u_groups[g][:, tiles, :], in_=hidden[g][:, tiles, :])
+            for j in range(GROUP_TILES):
+                nc.scalar.activation(out=hidden[g][:, j, :], in_=hidden[g][:, j, :], func=ACT.Gelu)
+                nc.sync.dma_start(out=u_groups[g][:, j, :], in_=hidden[g][:, j, :])
 
         W1_STEP = 2
         for step in range(-3, GROUPS + 5):

@@ -35,7 +35,6 @@ def tile_block_pb_t_kernel(tc, attn_out, x, W_proj, b_proj, g2, beta2, W1, b1, o
     x_mid_groups, u_groups = by_group(out_0), by_group(out_1)
 
     with ExitStack() as ctx:
-        ctx.enter_context(tc.manual_schedule())
         const = ctx.enter_context(tc.tile_pool(name="const", bufs=1))
         resident = ctx.enter_context(tc.tile_pool(name="resident", bufs=1))
         inputs = ctx.enter_context(tc.tile_pool(name="inputs", bufs=4))

@@ -22,6 +22,8 @@ GROUPS = TOKENS // GROUP_TOKENS
 STAT_COLS = GROUPS * GROUP_TILES
 LN_EPS = 1e-6
 
+BIAS_TILES_ON_GPSIMD = 1
+
 FLOPS = 2 * 2 * TOKENS * D * D
 
 
@@ -182,10 +184,17 @@ def tile_block_pb_t_kernel(tc, attn_out, x, W_proj, b_proj, g2, beta2, W1, b1, o
             if not 0 <= g < GROUPS:
                 return
             x_mid[g] = resident.tile([P, GROUP_TILES, D], F32, name="x_mid_%d" % g)
+            split = BIAS_TILES_ON_GPSIMD
+            nc.gpsimd.tensor_tensor(
+                out=x_mid[g][:, 0:split, :],
+                in0=x_rows[g][:, 0:split, :],
+                in1=bias_bcast[:, 0:1, :].to_broadcast([P, split, D]),
+                op=ALU.add,
+            )
             nc.vector.tensor_tensor(
-                out=x_mid[g][:],
-                in0=x_rows[g][:],
-                in1=bias_bcast[:, 0:1, :].to_broadcast([P, GROUP_TILES, D]),
+                out=x_mid[g][:, split:GROUP_TILES, :],
+                in0=x_rows[g][:, split:GROUP_TILES, :],
+                in1=bias_bcast[:, 0:1, :].to_broadcast([P, GROUP_TILES - split, D]),
                 op=ALU.add,
             )
 

from contextlib import ExitStack

import concourse.mybir as mybir
from concourse.masks import make_identity

F32 = mybir.dt.float32
BF16 = mybir.dt.bfloat16
U32 = mybir.dt.uint32
U8 = mybir.dt.uint8
FP8X4 = mybir.dt.float8_e4m3fn_x4
ALU = mybir.AluOpType
ACT = mybir.ActivationFunctionType

P = 128
PACK = 4
D = P * PACK
TOKENS = 4 * 1024
GROUP_TILES = 4
GROUP_TOKENS = GROUP_TILES * P
HALF = GROUP_TOKENS // 2
GROUPS = TOKENS // GROUP_TOKENS
STAT_COLS = GROUPS * GROUP_TILES
LN_EPS = 1e-6

BIAS_TILES_ON_GPSIMD = 1

FLOPS = 2 * 2 * TOKENS * D * D


def tile_block_pb_t_kernel(tc, attn_out, x, W_proj, b_proj, g2, beta2, W1, b1, out_0, out_1):
    nc = tc.nc

    def by_group(rows):
        return rows.flatten_outer_dims().rearrange("(g p j) d -> g p j d", p=P, j=GROUP_TILES)

    attn_groups, x_groups = by_group(attn_out), by_group(x)
    x_mid_groups, u_groups = by_group(out_0), by_group(out_1)

    with ExitStack() as ctx:
        const = ctx.enter_context(tc.tile_pool(name="const", bufs=1))
        resident = ctx.enter_context(tc.tile_pool(name="resident", bufs=1))
        inputs = ctx.enter_context(tc.tile_pool(name="inputs", bufs=4))
        pairs = ctx.enter_context(tc.tile_pool(name="pairs", bufs=2))
        triples = ctx.enter_context(tc.tile_pool(name="triples", bufs=3))
        flipped = ctx.enter_context(tc.psum_pool(name="flipped", bufs=4))
        sums = ctx.enter_context(tc.psum_pool(name="sums", bufs=4))

        attn_rows, x_rows = {}, {}

        def load(g):
            if not 0 <= g < GROUPS:
                return
            attn_rows[g] = inputs.tile([P, GROUP_TILES, D], BF16, name="attn_rows")
            nc.sync.dma_start(out=attn_rows[g][:], in_=attn_groups[g])
            x_rows[g] = inputs.tile([P, GROUP_TILES, D], BF16, name="x_rows")
            nc.sync.dma_start(out=x_rows[g][:], in_=x_groups[g])

        bias_rows = const.tile([P, 2, D], BF16)
        nc.vector.memset(bias_rows[:], 0.0)
        ln_rows = const.tile([P, P], BF16)
        nc.vector.memset(ln_rows[:], 0.0)
        nc.sync.dma_start(out=bias_rows[0:1, 0, :], in_=b_proj.rearrange("(o d) -> o d", o=1))
        nc.sync.dma_start(out=bias_rows[0:1, 1, :], in_=b1.rearrange("(o d) -> o d", o=1))
        nc.sync.dma_start(out=ln_rows[0:PACK, :], in_=g2.rearrange("(t p) -> t p", p=P))
        nc.sync.dma_start(out=ln_rows[PACK : 2 * PACK, :], in_=beta2.rearrange("(t p) -> t p", p=P))

        wp_rows = const.tile([P, PACK, D], BF16)
        nc.sync.dma_start(out=wp_rows[:], in_=W_proj.rearrange("(c p) k -> p c k", p=P))
        load(0)
        load(1)
        load(2)
        w1_rows = const.tile([P, PACK, D], BF16)
        nc.sync.dma_start(out=w1_rows[:], in_=W1.rearrange("(c p) k -> p c k", p=P))

        warm = const.tile([P, 1], F32)
        nc.vector.memset(warm[:], 0.0)
        nc.scalar.activation(out=warm[:], in_=warm[:], func=ACT.Gelu)

        ident_f32 = const.tile([P, P], F32)
        make_identity(nc, ident_f32[:])
        ident_bf16 = const.tile([P, P], BF16)
        make_identity(nc, ident_bf16[:])
        ones = const.tile([P, P], BF16)
        nc.vector.memset(ones[:], 1.0)
        neg_half = const.tile([P, GROUP_TILES], F32)
        nc.vector.memset(neg_half[:], -0.5)

        row_sum = const.tile([P, STAT_COLS], F32)
        neg_mean = const.tile([P, STAT_COLS], F32)
        sq_sum = const.tile([P, STAT_COLS], F32)
        var_eps = const.tile([P, STAT_COLS], F32)
        rstd = const.tile([P, STAT_COLS], F32)

        def stat_cols(g):
            return slice(g * GROUP_TILES, (g + 1) * GROUP_TILES)

        def stat_col(g, j):
            return slice(g * GROUP_TILES + j, g * GROUP_TILES + j + 1)

        bias_bcast = const.tile([P, 2, D], F32)
        for i in range(2):
            spread = sums.tile([P, D], F32, name="acc")
            nc.tensor.matmul(out=spread[:], lhsT=ones[:], rhs=bias_rows[:, i, :], start=True, stop=True)
            nc.scalar.copy(out=bias_bcast[:, i, :], in_=spread[:])

        ln_flipped = flipped.tile([P, P], BF16, name="bank")
        nc.tensor.transpose(ln_flipped[:], ln_rows[:], ident_bf16[:])
        ln_cols = const.tile([P, 2 * PACK], F32)
        nc.scalar.copy(out=ln_cols[:], in_=ln_flipped[:, 0 : 2 * PACK])

        def flip_words(rows):
            row_words = rows.bitcast(F32)
            banks = []
            for half in range(2):
                bank = flipped.tile([P, 2, HALF], F32, name="bank")
                for jj in range(2):
                    for u in range(2):
                        nc.tensor.transpose(
                            bank[:, u, jj * P : (jj + 1) * P],
                            row_words[:, 2 * half + jj, u * P : (u + 1) * P],
                            ident_f32[:],
                        )
                banks.append(bank)
            return banks

        def copy_words(banks, grouped):
            grouped_words = grouped.bitcast(F32)
            for half in range(2):
                nc.scalar.copy(
                    out=grouped_words[:, half * HALF : (half + 1) * HALF, :],
                    in_=banks[half][:].rearrange("p u w -> p w u"),
                )

        def quantise(grouped, operand):
            codes, scales = operand
            nc.vector.quantize_mx(
                out=codes[:].bitcast(FP8X4), scales=scales[:], in_=grouped.rearrange("p w t -> p (w t)")
            )

        def mx_operand(pool, name):
            codes = pool.tile([P, GROUP_TOKENS], U32, name=name + "_codes", align_bytes=64)
            scales = pool.tile([P, GROUP_TOKENS], U8, name=name + "_scales", align_bytes=64)
            return codes, scales

        def matmul_mx_tile(acc, tokens_operand, j, weight_operand):
            tokens = slice(j * P, (j + 1) * P)
            nc.tensor.matmul_mx(
                out=acc[:],
                lhsT=tokens_operand[0][:, tokens].bitcast(FP8X4),
                lhsT_scale=tokens_operand[1][:, tokens],
                rhs=weight_operand[0][:].bitcast(FP8X4),
                rhs_scale=weight_operand[1][:],
                start=True,
                stop=True,
            )

        wp_grouped = pairs.tile([P, D, PACK], BF16, name="a_grouped", align_bytes=64)
        copy_words(flip_words(wp_rows[:]), wp_grouped[:])
        wp_operand = mx_operand(const, "wp")
        quantise(wp_grouped[:], wp_operand)

        w1_operand = mx_operand(const, "w1")
        w1_grouped = const.tile([P, D, PACK], BF16, align_bytes=64)

        def flip_w1():
            for half in range(2):
                bank = flipped.tile([P, PACK, HALF], BF16, name="bank")
                for cc in range(2):
                    for t in range(PACK):
                        nc.tensor.transpose(
                            bank[:, t, cc * P : (cc + 1) * P],
                            w1_rows[:, 2 * half + cc, t * P : (t + 1) * P],
                            ident_bf16[:],
                        )
                nc.scalar.copy(
                    out=w1_grouped[:, half * HALF : (half + 1) * HALF, :],
                    in_=bank[:].rearrange("p t n -> p n t"),
                )

        a_banks, a_grouped, a_operand, x_mid = {}, {}, {}, {}
        normed, h_banks, h_planes, h_grouped, h_operand, hidden = {}, {}, {}, {}, {}, {}

        def add_bias(g):
            if not 0 <= g < GROUPS:
                return
            x_mid[g] = resident.tile([P, GROUP_TILES, D], F32, name="x_mid_%d" % g)
            split = BIAS_TILES_ON_GPSIMD
            nc.gpsimd.tensor_tensor(
                out=x_mid[g][:, 0:split, :],
                in0=x_rows[g][:, 0:split, :],
                in1=bias_bcast[:, 0:1, :].to_broadcast([P, split, D]),
                op=ALU.add,
            )
            nc.vector.tensor_tensor(
                out=x_mid[g][:, split:GROUP_TILES, :],
                in0=x_rows[g][:, split:GROUP_TILES, :],
                in1=bias_bcast[:, 0:1, :].to_broadcast([P, GROUP_TILES - split, D]),
                op=ALU.add,
            )

        def flip_attention(g):
            if not 0 <= g < GROUPS:
                return
            a_banks[g] = flip_words(attn_rows[g][:])

        def copy_attention(g):
            if not 0 <= g < GROUPS:
                return
            a_grouped[g] = pairs.tile([P, GROUP_TOKENS, PACK], BF16, name="a_grouped", align_bytes=64)
            copy_words(a_banks[g], a_grouped[g][:])

        def quantise_attention(g):
            if not 0 <= g < GROUPS:
                return
            a_operand[g] = mx_operand(triples, "a")
            quantise(a_grouped[g][:], a_operand[g])

        def project_attention(g):
            if not 0 <= g < GROUPS:
                return
            for j in range(GROUP_TILES):
                acc = sums.tile([P, D], F32, name="acc")
                matmul_mx_tile(acc, a_operand[g], j, wp_operand)
                nc.vector.scalar_tensor_tensor(
                    out=x_mid[g][:, j, :],
                    in0=acc[:],
                    scalar=1.0,
                    in1=x_mid[g][:, j, :],
                    op0=ALU.mult,
                    op1=ALU.add,
                    accum_out=row_sum[:, stat_col(g, j)],
                )

        def variance(g):
            if not 0 <= g < GROUPS:
                return
            nc.scalar.mul(out=neg_mean[:, stat_cols(g)], in_=row_sum[:, stat_cols(g)], mul=-1.0 / D)
            squares = pairs.tile([P, GROUP_TILES, D], BF16, name="squares")
            for j in range(GROUP_TILES):
                nc.scalar.activation(
                    out=squares[:, j, :],
                    in_=x_mid[g][:, j, :],
                    func=ACT.Square,
                    bias=neg_mean[:, stat_col(g, j)],
                    scale=1.0,
                    accum_out=sq_sum[:, stat_col(g, j)],
                )
            nc.sync.dma_start(out=x_mid_groups[g], in_=x_mid[g][:])

        def reciprocal_std(g):
            if not 0 <= g < GROUPS:
                return
            nc.gpsimd.tensor_scalar(
                out=var_eps[:, stat_cols(g)],
                in0=sq_sum[:, stat_cols(g)],
                scalar1=1.0 / D,
                scalar2=LN_EPS,
                op0=ALU.mult,
                op1=ALU.add,
            )
            nc.gpsimd.tensor_tensor(
                out=rstd[:, stat_cols(g)], in0=var_eps[:, stat_cols(g)], in1=neg_half[:], op=ALU.pow
            )

        def normalise(g):
            if not 0 <= g < GROUPS:
                return
            normed[g] = pairs.tile([P, GROUP_TILES, D], F32, name="normed")
            for j in range(GROUP_TILES):
                nc.vector.tensor_scalar(
                    out=normed[g][:, j, :],
                    in0=x_mid[g][:, j, :],
                    scalar1=neg_mean[:, stat_col(g, j)],
                    scalar2=rstd[:, stat_col(g, j)],
                    op0=ALU.add,
                    op1=ALU.mult,
                )

        def flip_normed(g):
            if not 0 <= g < GROUPS:
                return
            h_banks[g] = []
            for t in range(PACK):
                bank = flipped.tile([P, GROUP_TOKENS], F32, name="bank")
                for j in range(GROUP_TILES):
                    nc.tensor.transpose(
                        bank[:, j * P : (j + 1) * P], normed[g][:, j, t * P : (t + 1) * P], ident_f32[:]
                    )
                h_banks[g].append(bank)

        def scale_shift(g):
            if not 0 <= g < GROUPS:
                return
            h_planes[g] = pairs.tile([P, PACK, GROUP_TOKENS], BF16, name="h_planes")
            for t in range(PACK):
                nc.scalar.activation(
                    out=h_planes[g][:, t, :],
                    in_=h_banks[g][t][:],
                    func=ACT.Identity,
                    scale=ln_cols[:, t : t + 1],
                    bias=ln_cols[:, PACK + t : PACK + t + 1],
                )

        def regroup_h(g):
            if not 0 <= g < GROUPS:
                return
            h_grouped[g] = pairs.tile([P, GROUP_TOKENS, PACK], BF16, name="h_grouped", align_bytes=64)
            nc.vector.tensor_copy(
                out=h_grouped[g][:].rearrange("p (c i) t -> p c t i", i=4),
                in_=h_planes[g][:].rearrange("p t (c i) -> p c t i", i=4),
            )

        def quantise_h(g):
            if not 0 <= g < GROUPS:
                return
            h_operand[g] = mx_operand(triples, "h")
            quantise(h_grouped[g][:], h_operand[g])

        def project_h(g):
            if not 0 <= g < GROUPS:
                return
            hidden[g] = triples.tile([P, GROUP_TILES, D], F32, name="hidden")
            for j in range(GROUP_TILES):
                acc = sums.tile([P, D], F32, name="acc")
                matmul_mx_tile(acc, h_operand[g], j, w1_operand)
                nc.vector.tensor_tensor(
                    out=hidden[g][:, j, :], in0=acc[:], in1=bias_bcast[:, 1, :], op=ALU.add
                )

        def gelu(g):
            if not 0 <= g < GROUPS:
                return
            for j in range(GROUP_TILES):
                nc.scalar.activation(out=hidden[g][:, j, :], in_=hidden[g][:, j, :], func=ACT.Gelu)
                nc.sync.dma_start(out=u_groups[g][:, j, :], in_=hidden[g][:, j, :])

        W1_STEP = 2
        for step in range(-3, GROUPS + 5):
            project_attention(step)
            normalise(step - 1)
            project_h(step - 5)
            scale_shift(step - 2)
            copy_attention(step + 2)
            if step == W1_STEP:
                flip_w1()
            variance(step)
            quantise_h(step - 3)
            quantise_attention(step + 2)
            if step == W1_STEP + 1:
                quantise(w1_grouped[:], w1_operand)
            flip_normed(step - 1)
            gelu(step - 5)
            add_bias(step + 3)
            flip_attention(step + 3)
            reciprocal_std(step)
            regroup_h(step - 2)
            load(step + 6)
